import numpy as np
import ml_dtypes


def mxq(x, axis, fmt="e4m3"):
    dtype, down = {"e4m3": (ml_dtypes.float8_e4m3fn, 7), "e5m2": (ml_dtypes.float8_e5m2, 14)}[fmt]
    v = np.moveaxis(np.asarray(x, np.float32).astype(ml_dtypes.bfloat16).astype(np.float64), axis, -1)
    blocks = v.reshape(v.shape[:-1] + (-1, 32))
    amax = np.abs(blocks).max(-1, keepdims=True)
    byte = np.maximum(np.where(amax > 0, np.frexp(amax)[1] - 1 + 127, 0) - down, 1)
    scale = np.exp2(byte - 127.0)
    codes = (blocks / scale).astype(np.float32).astype(dtype).astype(np.float64)
    return np.moveaxis((codes * scale).reshape(v.shape), -1, axis)


WIDE = False


def mx_kscale(k):
    if not WIDE:
        return np.ones(k)
    levels = np.array([30, -30])
    if k % 512:
        return np.exp2(np.random.permutation(np.resize(levels, k // 32))).repeat(32)
    a = np.empty((k // 512, 16))
    for p in range(k // 512):
        a[p, :8] = np.random.permutation(np.resize(levels, 8))
        for g in range(8):
            far = levels[np.abs(levels - a[p, g]) >= 10]
            a[p, g + 8] = far[np.random.randint(len(far))]
    return np.exp2(a.ravel()).repeat(32)


BF16 = ml_dtypes.bfloat16


def bf(x):
    return np.asarray(x, np.float32).astype(BF16)


def f64(x):
    return np.asarray(x).astype(np.float64)


B, D, R = 2048, 2048, 128


def softplus(v):
    return np.log1p(np.exp(v))


def setup_inputs():
    s = mx_kscale(D)
    w = 1.0 / np.sqrt(D)
    return {"x": bf(np.random.standard_normal((B, D)) * s),
            "state_re": bf(np.random.standard_normal((B, R))),
            "state_im": bf(np.random.standard_normal((B, R))),
            "W_dt": bf(np.random.standard_normal((R, D)) * 0.5 * w / s),
            "b_dt": bf(np.random.standard_normal(R) * 0.3),
            "W_ph": bf(np.random.standard_normal((R, D)) * 0.5 * w / s),
            "b_ph": bf(np.random.standard_normal(R) * 0.3),
            "W_B": bf(np.random.standard_normal((R, D)) * w / s),
            "A_real": bf(np.random.standard_normal(R) * 0.5),
            "A_imag": bf(np.random.standard_normal(R) * 0.5)}


def reference(x, state_re, state_im, W_dt, b_dt, W_ph, b_ph, W_B, A_real, A_imag):
    xq = mxq(f64(x), 1, "e5m2")
    dt = softplus((xq @ mxq(f64(W_dt), 1, "e4m3").T) + f64(b_dt))
    phase = np.tanh((xq @ mxq(f64(W_ph), 1, "e4m3").T) + f64(b_ph)) * np.pi
    decay = np.exp(-dt * np.exp(f64(A_real)))
    angle = dt * f64(A_imag) + phase
    B_val = xq @ mxq(f64(W_B), 1, "e4m3").T
    cos = np.cos(angle)
    sin = np.sin(angle)
    new_re = (f64(state_re) * cos - f64(state_im) * sin) * decay + B_val
    new_im = (f64(state_re) * sin + f64(state_im) * cos) * decay
    return new_re, new_im

@@ -1,0 +1,310 @@
+import math
+from contextlib import ExitStack
+
+import concourse.mybir as mybir
+from concourse.masks import make_identity
+
+B, D, R = 2048, 2048, 128
+FLOPS = 2 * B * D * 3 * R
+
+F32 = mybir.dt.float32
+BF16 = mybir.dt.bfloat16
+I32 = mybir.dt.int32
+U32 = mybir.dt.uint32
+U8 = mybir.dt.uint8
+E4M3 = mybir.dt.float8_e4m3fn_x4
+E5M2 = mybir.dt.float8_e5m2_x4
+ACT = mybir.ActivationFunctionType
+ALU = mybir.AluOpType
+
+P = 128
+K_PASS = 512
+PASSES = D // K_PASS
+CHUNK = 512
+TILES = CHUNK // P
+CHUNKS = B // CHUNK
+UNITS = CHUNKS * PASSES
+EXP_CAP = 2.0 ** 50
+ROUND_EVEN = 1.5 * 2.0 ** 24
+COPY_ENG = "avavavaaaaaaaaaaaaaaavvvvvvvvaaaaaaaav"
+SCHED = {"7":"e:0 th:0 min:0","11":"e:1 th:1 min:1 ln:0 ln:1","13":"dt:0 dt:1 d:0-1","14":"st:0","15":"T:0-1","16":"e:2 th:2 n:0-1 r:0","17":"st:1 f:0-1 min:2","18":"r:1 abs:0-1","20":"e:3 th:3 B:0 B:1 B:2 B:3 min:3 ln:2 ln:3 vB:0 vB:1 vB:2 st:2 dt:2 dt:3 st:3 d:2 d:3 T:2-3 vB:3 n:2-3 r:2 f:2-3 S:0 C:0 S:1 C:1 r:3 p3:0 p4:0 oim:0 p2:0 p1:0 ore:0 abs:2 S:2 C:2 p3:1 p4:1 oim:1 p2:1 p1:1 ore:1 abs:3 S:3 C:3 xim:0 xre:0 p3:2 p4:2 oim:2 p2:2 p1:2 ore:2 xim:1 xre:1 p3:3 p4:3 oim:3 p2:3 p1:3 ore:3 xim:2 xre:2 xim:3 xre:3"}
+XBANKS = [0, 1, 2, 3]
+ZDT = [4,5,7,4]
+ZPH = [6,6,6,6]
+LATE = [[5,0,0,1],[5,1,2,3],[6,2,4,5],[7,3,6,7]]
+EVAC = 'aaaaaaaa'
+MXRUN = 1
+WB_AT = 10
+PERM = "---vvvvvvvv"
+Q_MODE = "cB"
+D_MODE = 'r'
+XBUFS = 3
+QBUFS = 6
+LOADS = "wdt x001 wph x011 x021 x031 x101 x111 x121 x131 wB x202 x222 s0 s1 x302 x322"
+RBUFS = 4
+
+
+def tile_mamba3mimoblock_pa_kernel(tc, x, state_re, state_im, W_dt, b_dt, W_ph, b_ph, W_B, A_real, A_imag, out_0, out_1):
+    nc = tc.nc
+    with ExitStack() as ctx:
+        keep = ctx.enter_context(tc.tile_pool(name="keep", bufs=1))
+        stage = ctx.enter_context(tc.tile_pool(name="stage", bufs=4))
+        late = ctx.enter_context(tc.tile_pool(name="late", bufs=2))
+        psum = ctx.enter_context(tc.psum_pool(name="psum", bufs=1))
+        ctx.enter_context(tc.manual_schedule())
+
+        def bank(index, shape, dtype):
+            return psum.tile(shape, dtype, name="bank%d" % index, tag="bank%d" % index)
+
+        w_raw = {}
+        x_raw = {}
+
+        def load_w(name, w):
+            w_raw[name] = stage.tile([P, D], BF16, name="raw_" + name, tag="quarter", bufs=QBUFS)
+            nc.sync.dma_start(out=w_raw[name][:], in_=w)
+
+        def load_x(c, g0, passes):
+            if passes == 1:
+                t = stage.tile([P, TILES, K_PASS], BF16, name="x_%d_%d" % (c, g0), tag="quarter", bufs=QBUFS)
+            else:
+                t = stage.tile([P, TILES, passes * K_PASS], BF16, name="x_half", bufs=XBUFS)
+            rows = x[c * CHUNK:(c + 1) * CHUNK, g0 * K_PASS:(g0 + passes) * K_PASS]
+            nc.sync.dma_start(out=t[:], in_=rows.rearrange("(p j) k -> p j k", j=TILES))
+            for g in range(passes):
+                x_raw[c, g0 + g] = t[:, :, g * K_PASS:(g + 1) * K_PASS]
+
+        ident_f32 = keep.tile([P, P], F32, name="ident_f32")
+        ident_bf16 = keep.tile([P, P], BF16, name="ident_bf16")
+        rows4 = keep.tile([P, P], BF16, name="rows4")
+        nc.vector.memset(rows4[:], 0.0)
+        make_identity(nc, ident_f32[:])
+        nc.vector.tensor_copy(out=ident_bf16[:], in_=ident_f32[:])
+        for i, vec in enumerate((b_dt, b_ph, A_real, A_imag)):
+            nc.scalar.dma_start(out=rows4[i:i + 1, :], in_=vec.rearrange("(o r) -> o r", o=1))
+
+        state = keep.tile([P, 2, CHUNKS, TILES, R], BF16, name="state")
+        for item in LOADS.split():
+            if item[0] == 'w':
+                load_w(item[1:], {'dt': W_dt, 'ph': W_ph, 'B': W_B}[item[1:]])
+            elif item[0] == 's':
+                part = int(item[1])
+                nc.sync.dma_start(out=state[:, part], in_=(state_re, state_im)[part].rearrange("(c p j) r -> p c j r", p=P, j=TILES))
+            else:
+                load_x(int(item[1]), int(item[2]), int(item[3]))
+
+        counter = [0]
+
+        def permute(source, eng):
+            t = stage.tile([P, 4, 2, P], F32, name="permuted", bufs=2)
+            src = source.bitcast(F32).rearrange("p s (w u) -> p s u w", u=2)
+            if eng == 'a':
+                nc.scalar.copy(out=t[:], in_=src)
+            else:
+                nc.vector.tensor_copy(out=t[:], in_=src)
+            return t
+
+        def turn(source, permuted=None):
+            grouped = stage.tile([P, 4 * P * 4], BF16, name="grouped", align_bytes=64)
+            words_out = grouped[:].bitcast(F32).rearrange("p (s r u) -> p s r u", s=4, u=2)
+            for half in range(2):
+                n = counter[0]
+                counter[0] = n + 1
+                xt = bank(XBANKS[n % len(XBANKS)], [P, 2, 2, P], F32)
+                for s in range(2):
+                    words = source[:, 2 * half + s, :].bitcast(F32)
+                    for u in range(2):
+                        nc.tensor.transpose(xt[:, s, u, :], words[:, u::2] if permuted is None else permuted[:, 2 * half + s, u, :], ident_f32[:])
+                src = xt[:].rearrange("p s u r -> p s r u")
+                dst = words_out[:, 2 * half:2 * half + 2]
+                if COPY_ENG[n] == 'a':
+                    nc.scalar.copy(out=dst, in_=src)
+                else:
+                    nc.vector.tensor_copy(out=dst, in_=src)
+            return grouped
+
+        def quantise(name, grouped, fmt):
+            codes = keep.tile([P, 4 * P], U32, name="codes_" + name, align_bytes=64)
+            scales = keep.tile([P, 4 * P], U8, name="scales_" + name, align_bytes=64)
+            nc.vector.quantize_mx(out=codes[:].bitcast(fmt), scales=scales[:], in_=grouped[:])
+            return codes, scales
+
+        wq = {}
+        xq = {}
+        z = {}
+
+        def product(name, c, g, index):
+            if g == 0:
+                z[name, c] = bank(index, [P, CHUNK], F32)
+            cols = slice(g * P, (g + 1) * P)
+            nc.tensor.matmul_mx(out=z[name, c][:], lhsT=wq[name][0][:, cols].bitcast(E4M3), lhsT_scale=wq[name][1][:, cols],
+                                rhs=xq[c, g][0][:].bitcast(E5M2), rhs_scale=xq[c, g][1][:], start=(g == 0), stop=(g == PASSES - 1))
+
+        def w_source(name):
+            return w_raw[name][:].rearrange("p (g k) -> p g k", g=PASSES)
+
+        consts = keep.tile([P, 8], F32, name="consts")
+        bias_dt, bias_ph, neg_rate, half_turns = consts[:, 0:1], consts[:, 1:2], consts[:, 4:5], consts[:, 5:6]
+
+        def channel_constants():
+            t = bank(ZPH[0], [P, P], BF16)
+            nc.tensor.transpose(t[:], rows4[:], ident_bf16[:])
+            nc.vector.tensor_copy(out=consts[:, 0:4], in_=t[:, 0:4])
+            nc.scalar.activation(out=consts[:, 6:7], in_=consts[:, 2:3], func=ACT.Exp)
+            nc.vector.tensor_scalar(out=half_turns, in0=consts[:, 3:4], scalar1=1.0 / math.pi, scalar2=None, op0=ALU.mult)
+            nc.vector.tensor_scalar(out=neg_rate, in0=consts[:, 6:7], scalar1=-1.0, scalar2=None, op0=ALU.mult)
+
+        soft = keep.tile([P, B], F32, name="soft")
+        step = keep.tile([P, B], F32, name="step")
+        turns = keep.tile([P, B], F32, name="turns")
+        whole = keep.tile([P, B], I32, name="whole")
+        sine = keep.tile([P, B], F32, name="sine")
+        cosine = keep.tile([P, B], F32, name="cosine")
+        decay = soft
+        work = {}
+
+        def cs(c0, c1=None):
+            return slice(c0 * CHUNK, ((c0 if c1 is None else c1) + 1) * CHUNK)
+
+        def do(what):
+            op, arg = what.split(':')
+            a = [int(v) for v in arg.split('-')]
+            c = a[0]
+            s = cs(*a)
+            if op == 'e':
+                nc.scalar.activation(out=soft[:, s], in_=z['dt', c][:], func=ACT.Exp, bias=bias_dt)
+            elif op == 'th':
+                nc.scalar.activation(out=turns[:, s], in_=z['ph', c][:], func=ACT.Tanh, bias=bias_ph)
+            elif op == 'min':
+                nc.vector.tensor_scalar(out=soft[:, s], in0=soft[:, s], scalar1=EXP_CAP, scalar2=None, op0=ALU.min)
+            elif op == 'ln':
+                nc.scalar.activation(out=soft[:, s], in_=soft[:, s], func=ACT.Ln, bias=1.0)
+            elif op == 'dt':
+                nc.vector.scalar_tensor_tensor(out=step[:, s], in0=z['dt', c][:], scalar=bias_dt, in1=soft[:, s], op0=ALU.add, op1=ALU.max)
+            elif op == 'T':
+                nc.vector.scalar_tensor_tensor(out=turns[:, s], in0=step[:, s], scalar=half_turns, in1=turns[:, s], op0=ALU.mult, op1=ALU.add)
+            elif op == 'n':
+                nc.vector.tensor_scalar(out=whole[:, s], in0=turns[:, s], scalar1=ROUND_EVEN, scalar2=ROUND_EVEN, op0=ALU.add, op1=ALU.subtract)
+            elif op == 'f':
+                nc.vector.tensor_tensor(out=turns[:, s], in0=turns[:, s], in1=whole[:, s], op=ALU.subtract)
+            elif op == 'd':
+                nc.scalar.activation(out=decay[:, s], in_=step[:, s], func=ACT.Exp, scale=neg_rate)
+            elif op == 'abs':
+                nc.scalar.activation(out=cosine[:, s], in_=turns[:, s], func=ACT.Abs)
+            elif op == 'vabs':
+                nc.vector.scalar_tensor_tensor(out=cosine[:, s], in0=turns[:, s], scalar=-1.0, in1=turns[:, s], op0=ALU.mult, op1=ALU.max)
+            elif op == 'S':
+                nc.scalar.activation(out=sine[:, s], in_=turns[:, s], func=ACT.Sin, scale=math.pi)
+            elif op == 'C':
+                nc.scalar.activation(out=cosine[:, s], in_=cosine[:, s], func=ACT.Sin, scale=-math.pi, bias=math.pi / 2)
+            elif op == 'st':
+                t = bank(LATE[c][0], [P, 2, TILES, P], BF16)
+                for part in range(2):
+                    for j in range(TILES):
+                        nc.tensor.transpose(t[:, part, j, :], state[:, part, c, j, :], ident_bf16[:])
+                work['st', c] = t
+            elif op == 'r':
+                r = late.tile([P, 2, CHUNK], F32, name="damped", bufs=RBUFS)
+                nc.vector.tensor_tensor(out=r[:], in0=work['st', c][:].rearrange("p a j t -> p a (j t)"),
+                                        in1=decay[:, s].unsqueeze(1).to_broadcast([P, 2, CHUNK]), op=ALU.mult)
+                work['r', c] = r
+            elif op == 'B':
+                for g in range(PASSES):
+                    product('B', c, g, LATE[c][1])
+            elif op == 'pS':
+                t = late.tile([P, 2, CHUNK], F32, name="by_sine")
+                src = work['r', c][:] if ('r', c) in work else work['st', c][:].rearrange("p a j t -> p a (j t)")
+                if Q_MODE == 'q':
+                    nc.vector.tensor_tensor(out=t[:], in0=src, in1=sine[:, s].unsqueeze(1).to_broadcast([P, 2, CHUNK]), op=ALU.mult)
+                else:
+                    nc.vector.tensor_tensor(out=t[:, 0, :], in0=src[:, 0, :], in1=sine[:, s], op=ALU.mult)
+                    nc.vector.scalar_tensor_tensor(out=t[:, 1, :], in0=src[:, 1, :], scalar=-1.0, in1=sine[:, s], op0=ALU.mult, op1=ALU.mult)
+                work['pS', c] = t
+            elif op == 'pC':
+                t = late.tile([P, 2, CHUNK], F32, name="by_cosine")
+                src = work['r', c][:] if ('r', c) in work else work['st', c][:].rearrange("p a j t -> p a (j t)")
+                nc.vector.tensor_tensor(out=t[:], in0=src, in1=cosine[:, s].unsqueeze(1).to_broadcast([P, 2, CHUNK]), op=ALU.mult)
+                work['pC', c] = t
+            elif op in ('p1', 'p2', 'p3', 'p4'):
+                if ('pS', c) not in work:
+                    work['pS', c] = late.tile([P, 2, CHUNK], F32, name="by_sine")
+                    work['pC', c] = late.tile([P, 2, CHUNK], F32, name="by_cosine")
+                src = work['r', c][:] if ('r', c) in work else work['st', c][:].rearrange("p a j t -> p a (j t)")
+                if op == 'p1':
+                    nc.vector.tensor_tensor(out=work['pC', c][:, 0, :], in0=src[:, 0, :], in1=cosine[:, s], op=ALU.mult)
+                elif op == 'p4':
+                    nc.vector.tensor_tensor(out=work['pC', c][:, 1, :], in0=src[:, 1, :], in1=cosine[:, s], op=ALU.mult)
+                elif op == 'p3':
+                    nc.vector.tensor_tensor(out=work['pS', c][:, 0, :], in0=src[:, 0, :], in1=sine[:, s], op=ALU.mult)
+                else:
+                    nc.vector.scalar_tensor_tensor(out=work['pS', c][:, 1, :], in0=src[:, 1, :], scalar=-1.0, in1=sine[:, s], op0=ALU.mult, op1=ALU.mult)
+            elif op == 'q':
+                t = work['pS', c]
+                nc.vector.tensor_tensor(out=t[:, 1, :], in0=z['B', c][:], in1=t[:, 1, :], op=ALU.subtract)
+            elif op == 'cB' or op == 'vB':
+                t = late.tile([P, CHUNK], F32, name="b_val", bufs=4)
+                if op == 'cB':
+                    nc.scalar.copy(out=t[:], in_=z['B', c][:])
+                else:
+                    nc.vector.tensor_copy(out=t[:], in_=z['B', c][:])
+                work['cB', c] = t
+            elif op == 'gS':
+                nc.gpsimd.tensor_tensor(out=sine[:, s], in0=sine[:, s], in1=decay[:, s], op=ALU.mult)
+            elif op == 'gC':
+                nc.gpsimd.tensor_tensor(out=cosine[:, s], in0=cosine[:, s], in1=decay[:, s], op=ALU.mult)
+            elif op == 'vS':
+                nc.vector.tensor_tensor(out=sine[:, s], in0=sine[:, s], in1=decay[:, s], op=ALU.mult)
+            elif op == 'vC':
+                nc.vector.tensor_tensor(out=cosine[:, s], in0=cosine[:, s], in1=decay[:, s], op=ALU.mult)
+            elif op == 'ore' or op == 'oim':
+                part = 0 if op == 'ore' else 1
+                t = bank(LATE[c][2 + part], [P, TILES, P], F32)
+                for j in range(TILES):
+                    tok = slice(j * P, (j + 1) * P)
+                    with_b = part == 0 and ('cB', c) in work
+                    if with_b:
+                        nc.tensor.matmul(t[:, j, :], lhsT=work['cB', c][:, tok], rhs=ident_f32[:], start=True, stop=False, is_transpose=True)
+                    nc.tensor.matmul(t[:, j, :], lhsT=work['pS', c][:, 1 - part, tok], rhs=ident_f32[:], start=not with_b, stop=False, is_transpose=True)
+                    nc.tensor.matmul(t[:, j, :], lhsT=work['pC', c][:, part, tok], rhs=ident_f32[:], start=False, stop=True, is_transpose=True)
+                work[op, c] = t
+            elif op == 'xre' or op == 'xim':
+                part = 0 if op == 'xre' else 1
+                res = late.tile([P, TILES, R], F32, name="result%d" % part)
+                src = work['o' + op[1:], c]
+                if EVAC[2 * c + part] == 'a':
+                    nc.scalar.copy(out=res[:], in_=src[:])
+                else:
+                    nc.vector.tensor_copy(out=res[:], in_=src[:])
+                dst = (out_0, out_1)[part][c * CHUNK:(c + 1) * CHUNK, :]
+                nc.sync.dma_start(out=dst.rearrange("(p j) r -> p j r", j=TILES), in_=res[:])
+            else:
+                raise ValueError(op)
+
+        seq = [('dt',), (0, 0), ('ph',)] + [divmod(i, PASSES) for i in range(1, UNITS)]
+        seq = seq[:WB_AT] + [('B',)] + seq[WB_AT:]
+        def src_of(item):
+            return w_source(item[0]) if len(item) == 1 else x_raw[item]
+        perm = {}
+        grouped = {}
+        pending = []
+        for i in range(-1, len(seq) + 2):
+            if i + 1 < len(seq) and i + 1 < len(PERM) and PERM[i + 1] != '-':
+                perm[i + 1] = permute(src_of(seq[i + 1]), PERM[i + 1])
+            if 0 <= i < len(seq):
+                grouped[i] = turn(src_of(seq[i]), perm.get(i))
+            if 0 <= i - 1 < len(seq):
+                item = seq[i - 1]
+                if len(item) == 1:
+                    wq[item[0]] = quantise("w_" + item[0], grouped[i - 1], E4M3)
+                else:
+                    xq[item] = quantise("x_%d_%d" % item, grouped[i - 1], E5M2)
+            if i == 3:
+                channel_constants()
+            if 0 <= i - 2 < len(seq) and len(seq[i - 2]) == 2:
+                pending.append(seq[i - 2])
+            if i >= 4 and (len(pending) >= MXRUN or i >= len(seq)):
+                for c, g in pending:
+                    product("dt", c, g, ZDT[c])
+                    product("ph", c, g, ZPH[c])
+                pending = []
+            for what in SCHED.get(str(i), '').split():
+                do(what)

@@ -26,21 +26,25 @@ CHUNKS = B // CHUNK
 UNITS = CHUNKS * PASSES
 EXP_CAP = 2.0 ** 50
 ROUND_EVEN = 1.5 * 2.0 ** 24
-COPY_ENG = "avavavaaaaaaaaaaaaaaavvvvvvvvaaaaaaaav"
-SCHED = {"7":"e:0 th:0 min:0","11":"e:1 th:1 min:1 ln:0 ln:1","13":"dt:0 dt:1 d:0-1","14":"st:0","15":"T:0-1","16":"e:2 th:2 n:0-1 r:0","17":"st:1 f:0-1 min:2","18":"r:1 abs:0-1","20":"e:3 th:3 B:0 B:1 B:2 B:3 min:3 ln:2 ln:3 vB:0 vB:1 vB:2 st:2 dt:2 dt:3 st:3 d:2 d:3 T:2-3 vB:3 n:2-3 r:2 f:2-3 S:0 C:0 S:1 C:1 r:3 p3:0 p4:0 oim:0 p2:0 p1:0 ore:0 abs:2 S:2 C:2 p3:1 p4:1 oim:1 p2:1 p1:1 ore:1 abs:3 S:3 C:3 xim:0 xre:0 p3:2 p4:2 oim:2 p2:2 p1:2 ore:2 xim:1 xre:1 p3:3 p4:3 oim:3 p2:3 p1:3 ore:3 xim:2 xre:2 xim:3 xre:3"}
+COPY_ENG = "aaaaaaaaaaaaaaaaaaaaaavvvvvvaaaaaaavvv"
+SCHED = {"7":"e:0 th:0 min:0","11":"e:1 th:1 min:1 ln:0 ln:1","13":"dt:0 dt:1 d:0-1","14":"st:0 T:0-1","15":"e:2 th:2 n:0-1 r:0","16":"st:1 f:0-1 min:2","17":"r:1 abs:0-1","19":"e:3 th:3 min:3 ln:2 ln:3 st:2 st:3 dt:2 dt:3 d:2 d:3 B:0 B:1 T:2-3 r:2 n:2-3 r:3 f:2-3 S:0 C:0 S:1 C:1 p3:0 p4:0 oim:0 p2:0 p1:0 q:0 ore:0 abs:2 S:2 C:2 B:2 p3:1 p4:1 oim:1 p2:1 p1:1 q:1 ore:1 abs:3 S:3 C:3 xim:0 xre:0 B:3 p3:2 p4:2 oim:2 p2:2 p1:2 q:2 ore:2 xim:1 xre:1 p3:3 p4:3 oim:3 p2:3 p1:3 q:3 ore:3 xim:2 xre:2 xim:3 xre:3"}
 XBANKS = [0, 1, 2, 3]
 ZDT = [4,5,7,4]
 ZPH = [6,6,6,6]
-LATE = [[5,0,0,1],[5,1,2,3],[6,2,4,5],[7,3,6,7]]
+LATE = [[5,7,0,1],[5,4,2,3],[6,6,0,1],[5,5,2,3]]
 EVAC = 'aaaaaaaa'
 MXRUN = 1
-WB_AT = 10
-PERM = "---vvvvvvvv"
-Q_MODE = "cB"
+WB_AT = 18
+PERM = "vvvvvvvvvv"
+Q_MODE = "q"
 D_MODE = 'r'
 XBUFS = 3
+PIN = 'all'
+MIX = []
+QFIRST = [10,18]
+CONST_AT = 5
 QBUFS = 6
-LOADS = "wdt x001 wph x011 x021 x031 x101 x111 x121 x131 wB x202 x222 s0 s1 x302 x322"
+LOADS = "wdt x001 wph x011 x021 x031 x101 x111 x121 x131 x202 x222 s0 s1 x302 x322 wB"
 RBUFS = 4
 
 
@@ -51,7 +55,10 @@ def tile_mamba3mimoblock_pa_kernel(tc, x, state_re, state_im, W_dt, b_dt, W_ph, 
         stage = ctx.enter_context(tc.tile_pool(name="stage", bufs=4))
         late = ctx.enter_context(tc.tile_pool(name="late", bufs=2))
         psum = ctx.enter_context(tc.psum_pool(name="psum", bufs=1))
-        ctx.enter_context(tc.manual_schedule())
+        if PIN == 'all':
+            ctx.enter_context(tc.manual_schedule())
+        else:
+            ctx.enter_context(tc.manual_schedule(engines={mybir.EngineType.Activation, mybir.EngineType.PE, mybir.EngineType.SP}))
 
         def bank(index, shape, dtype):
             return psum.tile(shape, dtype, name="bank%d" % index, tag="bank%d" % index)
@@ -146,7 +153,7 @@ def tile_mamba3mimoblock_pa_kernel(tc, x, state_re, state_im, W_dt, b_dt, W_ph, 
         bias_dt, bias_ph, neg_rate, half_turns = consts[:, 0:1], consts[:, 1:2], consts[:, 4:5], consts[:, 5:6]
 
         def channel_constants():
-            t = bank(ZPH[0], [P, P], BF16)
+            t = bank(7, [P, P], BF16)
             nc.tensor.transpose(t[:], rows4[:], ident_bf16[:])
             nc.vector.tensor_copy(out=consts[:, 0:4], in_=t[:, 0:4])
             nc.scalar.activation(out=consts[:, 6:7], in_=consts[:, 2:3], func=ACT.Exp)
@@ -184,6 +191,12 @@ def tile_mamba3mimoblock_pa_kernel(tc, x, state_re, state_im, W_dt, b_dt, W_ph, 
                 nc.vector.scalar_tensor_tensor(out=turns[:, s], in0=step[:, s], scalar=half_turns, in1=turns[:, s], op0=ALU.mult, op1=ALU.add)
             elif op == 'n':
                 nc.vector.tensor_scalar(out=whole[:, s], in0=turns[:, s], scalar1=ROUND_EVEN, scalar2=ROUND_EVEN, op0=ALU.add, op1=ALU.subtract)
+            elif op == 'an':
+                nc.scalar.activation(out=whole[:, s].bitcast(U32), in_=turns[:, s], func=ACT.Copy, bias=ROUND_EVEN)
+            elif op == 'fa':
+                nc.vector.scalar_tensor_tensor(out=turns[:, s], in0=whole[:, s], scalar=ROUND_EVEN, in1=turns[:, s], op0=ALU.subtract, op1=ALU.subtract)
+                for v in range(a[0], a[-1] + 1):
+                    work['neg', v] = True
             elif op == 'f':
                 nc.vector.tensor_tensor(out=turns[:, s], in0=turns[:, s], in1=whole[:, s], op=ALU.subtract)
             elif op == 'd':
@@ -193,7 +206,7 @@ def tile_mamba3mimoblock_pa_kernel(tc, x, state_re, state_im, W_dt, b_dt, W_ph, 
             elif op == 'vabs':
                 nc.vector.scalar_tensor_tensor(out=cosine[:, s], in0=turns[:, s], scalar=-1.0, in1=turns[:, s], op0=ALU.mult, op1=ALU.max)
             elif op == 'S':
-                nc.scalar.activation(out=sine[:, s], in_=turns[:, s], func=ACT.Sin, scale=math.pi)
+                nc.scalar.activation(out=sine[:, s], in_=turns[:, s], func=ACT.Sin, scale=-math.pi if ('neg', c) in work else math.pi)
             elif op == 'C':
                 nc.scalar.activation(out=cosine[:, s], in_=cosine[:, s], func=ACT.Sin, scale=-math.pi, bias=math.pi / 2)
             elif op == 'st':
@@ -235,8 +248,45 @@ def tile_mamba3mimoblock_pa_kernel(tc, x, state_re, state_im, W_dt, b_dt, W_ph, 
                     nc.vector.tensor_tensor(out=work['pC', c][:, 1, :], in0=src[:, 1, :], in1=cosine[:, s], op=ALU.mult)
                 elif op == 'p3':
                     nc.vector.tensor_tensor(out=work['pS', c][:, 0, :], in0=src[:, 0, :], in1=sine[:, s], op=ALU.mult)
+                elif ('cB', c) not in work:
+                    nc.vector.tensor_tensor(out=work['pS', c][:, 1, :], in0=src[:, 1, :], in1=sine[:, s], op=ALU.mult)
                 else:
                     nc.vector.scalar_tensor_tensor(out=work['pS', c][:, 1, :], in0=src[:, 1, :], scalar=-1.0, in1=sine[:, s], op0=ALU.mult, op1=ALU.mult)
+            elif op in ('Td', 'TS', 'TC'):
+                src = {'Td': decay, 'TS': sine, 'TC': cosine}[op]
+                t = bank(MIX[c][('Td', 'TS', 'TC').index(op)], [P, TILES, P], F32)
+                for j in range(TILES):
+                    nc.tensor.transpose(t[:, j, :], src[:, c * CHUNK + j * P:c * CHUNK + (j + 1) * P], ident_f32[:])
+                work[op, c] = t
+            elif op == 'Bt':
+                t = bank(MIX[c][3], [P, TILES, P], F32)
+                for j in range(TILES):
+                    tok = slice(j * P, (j + 1) * P)
+                    for g in range(PASSES):
+                        cols = slice(g * P, (g + 1) * P)
+                        nc.tensor.matmul_mx(out=t[:, j, :], lhsT=xq[c, g][0][:, tok].bitcast(E5M2), lhsT_scale=xq[c, g][1][:, tok],
+                                            rhs=wq['B'][0][:, cols].bitcast(E4M3), rhs_scale=wq['B'][1][:, cols], start=(g == 0), stop=(g == PASSES - 1))
+                work[op, c] = t
+            elif op == 'rt':
+                r = late.tile([P, 2, CHUNK], F32, name="damped", bufs=RBUFS)
+                nc.vector.tensor_tensor(out=r[:], in0=work['Td', c][:].rearrange("p j t -> p (j t)").unsqueeze(1).to_broadcast([P, 2, CHUNK]),
+                                        in1=state[:, :, c].rearrange("p a j r -> p a (j r)"), op=ALU.mult)
+                work['r', c] = r
+            elif op == 'mS' or op == 'mC':
+                t = late.tile([P, 2, CHUNK], F32, name="by_sine" if op == 'mS' else "by_cosine")
+                nc.vector.tensor_tensor(out=t[:], in0=work['T' + op[1], c][:].rearrange("p j t -> p (j t)").unsqueeze(1).to_broadcast([P, 2, CHUNK]),
+                                        in1=work['r', c][:], op=ALU.mult)
+                work['p' + op[1], c] = t
+            elif op == 'mq':
+                t = work['pS', c]
+                nc.vector.tensor_tensor(out=t[:, 1, :], in0=work['Bt', c][:].rearrange("p j t -> p (j t)"), in1=t[:, 1, :], op=ALU.subtract)
+            elif op in ('gre', 'gim', 'vre', 'vim'):
+                part = 0 if op[1:] == 're' else 1
+                res = late.tile([P, CHUNK], F32, name="result%d" % part)
+                eng = nc.gpsimd if op[0] == 'g' else nc.vector
+                eng.tensor_tensor(out=res[:], in0=work['pS', c][:, 1 - part, :], in1=work['pC', c][:, part, :], op=ALU.add)
+                dst = (out_0, out_1)[part][c * CHUNK:(c + 1) * CHUNK, :]
+                nc.sync.dma_start(out=dst.rearrange("(p j) r -> p (j r)", j=TILES), in_=res[:])
             elif op == 'q':
                 t = work['pS', c]
                 nc.vector.tensor_tensor(out=t[:, 1, :], in0=z['B', c][:], in1=t[:, 1, :], op=ALU.subtract)
@@ -289,7 +339,7 @@ def tile_mamba3mimoblock_pa_kernel(tc, x, state_re, state_im, W_dt, b_dt, W_ph, 
         for i in range(-1, len(seq) + 2):
             if i + 1 < len(seq) and i + 1 < len(PERM) and PERM[i + 1] != '-':
                 perm[i + 1] = permute(src_of(seq[i + 1]), PERM[i + 1])
-            if 0 <= i < len(seq):
+            if 0 <= i < len(seq) and i not in QFIRST:
                 grouped[i] = turn(src_of(seq[i]), perm.get(i))
             if 0 <= i - 1 < len(seq):
                 item = seq[i - 1]
@@ -297,7 +347,9 @@ def tile_mamba3mimoblock_pa_kernel(tc, x, state_re, state_im, W_dt, b_dt, W_ph, 
                     wq[item[0]] = quantise("w_" + item[0], grouped[i - 1], E4M3)
                 else:
                     xq[item] = quantise("x_%d_%d" % item, grouped[i - 1], E5M2)
-            if i == 3:
+            if 0 <= i < len(seq) and i in QFIRST:
+                grouped[i] = turn(src_of(seq[i]), perm.get(i))
+            if i == CONST_AT:
                 channel_constants()
             if 0 <= i - 2 < len(seq) and len(seq[i - 2]) == 2:
                 pending.append(seq[i - 2])

@@ -26,25 +26,26 @@ CHUNKS = B // CHUNK
 UNITS = CHUNKS * PASSES
 EXP_CAP = 2.0 ** 50
 ROUND_EVEN = 1.5 * 2.0 ** 24
-COPY_ENG = "aaaaaaaaaaaaaaaaaaaaaavvvvvvaaaaaaavvv"
-SCHED = {"7":"e:0 th:0 min:0","11":"e:1 th:1 min:1 ln:0 ln:1","13":"dt:0 dt:1 d:0-1","14":"st:0 T:0-1","15":"e:2 th:2 n:0-1 r:0","16":"st:1 f:0-1 min:2","17":"r:1 abs:0-1","19":"e:3 th:3 min:3 ln:2 ln:3 st:2 st:3 dt:2 dt:3 d:2 d:3 B:0 B:1 T:2-3 r:2 n:2-3 r:3 f:2-3 S:0 C:0 S:1 C:1 p3:0 p4:0 oim:0 p2:0 p1:0 q:0 ore:0 abs:2 S:2 C:2 B:2 p3:1 p4:1 oim:1 p2:1 p1:1 q:1 ore:1 abs:3 S:3 C:3 xim:0 xre:0 B:3 p3:2 p4:2 oim:2 p2:2 p1:2 q:2 ore:2 xim:1 xre:1 p3:3 p4:3 oim:3 p2:3 p1:3 q:3 ore:3 xim:2 xre:2 xim:3 xre:3"}
+COPY_ENG = 'avavav' + 'av' * 16
+SCHED = {}
 XBANKS = [0, 1, 2, 3]
 ZDT = [4,5,7,4]
-ZPH = [6,6,6,6]
-LATE = [[5,7,0,1],[5,4,2,3],[6,6,0,1],[5,5,2,3]]
+ZPH = [6,6,6,5]
+LATE = [[0,6,0,1],[1,5,2,3],[2,7,0,1],[3,4,2,3]]
 EVAC = 'aaaaaaaa'
 MXRUN = 1
-WB_AT = 18
-PERM = "vvvvvvvvvv"
-Q_MODE = "q"
+WB_AT = 99
+PERM = ''
+Q_MODE = 'q'
 D_MODE = 'r'
-XBUFS = 3
+XBUFS = 4
+ORDER = "L:wdt L:x0 L:wph L:x1 L:x2 L:x3 L:x4 L:x5 P:dt P:0 Ta:dt aa:dt Tb:dt ab:dt L:x6 P:ph Ta:0 aa:0 Tb:0 ab:0 Q:dt L:x7 P:1 Ta:ph aa:ph Tb:ph ab:ph Q:0 L:x8 P:2 Ta:1 aa:1 Tb:1 ab:1 Q:ph L:x9 L:s0 L:s1 K:0 P:3 Ta:2 aa:2 Tb:2 ab:2 Q:1 L:x10 Md:0 Mp:0 P:4 Ta:3 aa:3 Tb:3 ab:3 Q:2 L:x11 Md:1 Mp:1 P:5 Ta:4 aa:4 Tb:4 ab:4 Q:3 L:x12 Md:2 Mp:2 P:6 Ta:5 aa:5 Tb:5 ab:5 Q:4 L:x13 Md:3 Mp:3 e:0 th:0 min:0 P:7 Ta:6 aa:6 Tb:6 ab:6 Q:5 L:x14 Md:4 Mp:4 P:8 Ta:7 aa:7 Tb:7 ab:7 Q:6 L:x15 Md:5 Mp:5 P:9 Q:7 Ta:8 aa:8 Tb:8 ab:8 L:wB Md:6 Mp:6 Ta:9 va:9 Tb:9 ab:9 Q:8 Md:7 Mp:7 e:1 th:1 Ta:10 va:10 Tb:10 ab:10 Q:9 Md:8 Mp:8 min:1 ln:0 Ta:11 va:11 Tb:11 ab:11 Q:10 Md:9 Mp:9 ln:1 dt:0 Ta:12 va:12 Tb:12 ab:12 Q:11 Md:10 Mp:10 dt:1 d:0 Ta:13 va:13 Tb:13 ab:13 Q:12 Md:11 Mp:11 T:0 d:1 e:2 Ta:14 va:14 Tb:14 ab:14 Q:13 Md:12 Mp:12 T:1 th:2 min:2 n:0-1 Ta:15 va:15 Tb:15 ab:15 Q:14 Md:13 Mp:13 Q:15 Ta:B aa:B Tb:B ab:B Md:14 Mp:14 Q:B Md:15 Mp:15 e:3 th:3 st:0 st:1 st:2 st:3 B:0 B:1 f:0-1 min:3 r:0 ln:2 ln:3 r:1 dt:2 dt:3 B:2 B:3 d:2 d:3 T:2 T:3 n:2 n:3 r:2 f:2-3 S:0 abs:0 S:1 C:0 abs:1 C:1 r:3 pS:0 pC:0 oim:0 q:0 ore:0 S:2 abs:2 S:3 C:2 abs:3 C:3 pS:1 pC:1 oim:1 q:1 ore:1 xim:0 xre:0 pS:2 pC:2 oim:2 q:2 ore:2 xim:1 xre:1 p2:3 p1:3 q:3 ore:3 p3:3 p4:3 oim:3 xim:2 xre:2 xre:3 xim:3"
 PIN = 'all'
 MIX = []
-QFIRST = [10,18]
-CONST_AT = 5
-QBUFS = 6
-LOADS = "wdt x001 wph x011 x021 x031 x101 x111 x121 x131 x202 x222 s0 s1 x302 x322 wB"
+QFIRST = []
+CONST_AT = 3
+QBUFS = 8
+LOADS = ''
 RBUFS = 4
 
 
@@ -70,15 +71,11 @@ def tile_mamba3mimoblock_pa_kernel(tc, x, state_re, state_im, W_dt, b_dt, W_ph, 
             w_raw[name] = stage.tile([P, D], BF16, name="raw_" + name, tag="quarter", bufs=QBUFS)
             nc.sync.dma_start(out=w_raw[name][:], in_=w)
 
-        def load_x(c, g0, passes):
-            if passes == 1:
-                t = stage.tile([P, TILES, K_PASS], BF16, name="x_%d_%d" % (c, g0), tag="quarter", bufs=QBUFS)
-            else:
-                t = stage.tile([P, TILES, passes * K_PASS], BF16, name="x_half", bufs=XBUFS)
-            rows = x[c * CHUNK:(c + 1) * CHUNK, g0 * K_PASS:(g0 + passes) * K_PASS]
-            nc.sync.dma_start(out=t[:], in_=rows.rearrange("(p j) k -> p j k", j=TILES))
-            for g in range(passes):
-                x_raw[c, g0 + g] = t[:, :, g * K_PASS:(g + 1) * K_PASS]
+        def load_x(i):
+            c, j = divmod(i, TILES)
+            x_raw[i] = stage.tile([P, D], BF16, name="x_%d" % i, tag="quarter", bufs=QBUFS)
+            rows = x[c * CHUNK:(c + 1) * CHUNK, :].rearrange("(p j) k -> j p k", j=TILES)
+            nc.sync.dma_start(out=x_raw[i][:], in_=rows[j])
 
         ident_f32 = keep.tile([P, P], F32, name="ident_f32")
         ident_bf16 = keep.tile([P, P], BF16, name="ident_bf16")
@@ -90,14 +87,15 @@ def tile_mamba3mimoblock_pa_kernel(tc, x, state_re, state_im, W_dt, b_dt, W_ph, 
             nc.scalar.dma_start(out=rows4[i:i + 1, :], in_=vec.rearrange("(o r) -> o r", o=1))
 
         state = keep.tile([P, 2, CHUNKS, TILES, R], BF16, name="state")
-        for item in LOADS.split():
+
+        def load(item):
             if item[0] == 'w':
                 load_w(item[1:], {'dt': W_dt, 'ph': W_ph, 'B': W_B}[item[1:]])
             elif item[0] == 's':
                 part = int(item[1])
                 nc.sync.dma_start(out=state[:, part], in_=(state_re, state_im)[part].rearrange("(c p j) r -> p c j r", p=P, j=TILES))
             else:
-                load_x(int(item[1]), int(item[2]), int(item[3]))
+                load_x(int(item[1:]))
 
         counter = [0]
 
@@ -110,24 +108,38 @@ def tile_mamba3mimoblock_pa_kernel(tc, x, state_re, state_im, W_dt, b_dt, W_ph, 
                 nc.vector.tensor_copy(out=t[:], in_=src)
             return t
 
-        def turn(source, permuted=None):
-            grouped = stage.tile([P, 4 * P * 4], BF16, name="grouped", align_bytes=64)
-            words_out = grouped[:].bitcast(F32).rearrange("p (s r u) -> p s r u", s=4, u=2)
-            for half in range(2):
-                n = counter[0]
-                counter[0] = n + 1
-                xt = bank(XBANKS[n % len(XBANKS)], [P, 2, 2, P], F32)
-                for s in range(2):
-                    words = source[:, 2 * half + s, :].bitcast(F32)
-                    for u in range(2):
-                        nc.tensor.transpose(xt[:, s, u, :], words[:, u::2] if permuted is None else permuted[:, 2 * half + s, u, :], ident_f32[:])
-                src = xt[:].rearrange("p s u r -> p s r u")
-                dst = words_out[:, 2 * half:2 * half + 2]
-                if COPY_ENG[n] == 'a':
-                    nc.scalar.copy(out=dst, in_=src)
-                else:
-                    nc.vector.tensor_copy(out=dst, in_=src)
-            return grouped
+        grouped = {}
+        perm = {}
+        turned = {}
+
+        def src_of(item):
+            raw = w_raw[item] if item in w_raw else x_raw[int(item)]
+            return raw[:].rearrange("p (g k) -> p g k", g=PASSES)
+
+        def turn(item, half):
+            n = counter[0]
+            counter[0] = n + 1
+            xt = bank(XBANKS[n % len(XBANKS)], [P, 2, 2, P], F32)
+            for s in range(2):
+                for u in range(2):
+                    if item in perm:
+                        nc.tensor.transpose(xt[:, s, u, :], perm[item][:, 2 * half + s, u, :], ident_f32[:])
+                    else:
+                        words = src_of(item)[:, 2 * half + s, :].bitcast(F32)
+                        nc.tensor.transpose(xt[:, s, u, :], words[:, u::2], ident_f32[:])
+            turned[item, half] = xt
+
+        def evacuate(item, half, eng):
+            if item not in grouped:
+                grouped[item] = stage.tile([P, 4 * P * 4], BF16, name="grouped", align_bytes=64)
+            words_out = grouped[item][:].bitcast(F32).rearrange("p (s r u) -> p s r u", s=4, u=2)
+            src = turned[item, half][:].rearrange("p s u r -> p s r u")
+            dst = words_out[:, 2 * half:2 * half + 2]
+            if eng == 'a':
+                nc.scalar.copy(out=dst, in_=src)
+            else:
+                nc.vector.tensor_copy(out=dst, in_=src)
+            turned[item, half, 'done'] = True
 
         def quantise(name, grouped, fmt):
             codes = keep.tile([P, 4 * P], U32, name="codes_" + name, align_bytes=64)
@@ -136,15 +148,19 @@ def tile_mamba3mimoblock_pa_kernel(tc, x, state_re, state_im, W_dt, b_dt, W_ph, 
             return codes, scales
 
         wq = {}
+        work = {}
         xq = {}
         z = {}
 
-        def product(name, c, g, index):
-            if g == 0:
+        def product(name, i, index):
+            c, j = divmod(i, TILES)
+            if (name, c) not in z:
                 z[name, c] = bank(index, [P, CHUNK], F32)
-            cols = slice(g * P, (g + 1) * P)
-            nc.tensor.matmul_mx(out=z[name, c][:], lhsT=wq[name][0][:, cols].bitcast(E4M3), lhsT_scale=wq[name][1][:, cols],
-                                rhs=xq[c, g][0][:].bitcast(E5M2), rhs_scale=xq[c, g][1][:], start=(g == 0), stop=(g == PASSES - 1))
+            for g in range(PASSES):
+                cols = slice(g * P, (g + 1) * P)
+                nc.tensor.matmul_mx(out=z[name, c][:, j * P:(j + 1) * P], lhsT=wq[name][0][:, cols].bitcast(E4M3), lhsT_scale=wq[name][1][:, cols],
+                                    rhs=xq[i][0][:, cols].bitcast(E5M2), rhs_scale=xq[i][1][:, cols], start=(g == 0), stop=(g == PASSES - 1))
+            work[name, 'n', c] = work.get((name, 'n', c), 0) + 1
 
         def w_source(name):
             return w_raw[name][:].rearrange("p (g k) -> p g k", g=PASSES)
@@ -167,16 +183,55 @@ def tile_mamba3mimoblock_pa_kernel(tc, x, state_re, state_im, W_dt, b_dt, W_ph, 
         sine = keep.tile([P, B], F32, name="sine")
         cosine = keep.tile([P, B], F32, name="cosine")
         decay = soft
-        work = {}
 
         def cs(c0, c1=None):
             return slice(c0 * CHUNK, ((c0 if c1 is None else c1) + 1) * CHUNK)
 
         def do(what):
             op, arg = what.split(':')
+            if op == 'L':
+                load(arg)
+                return
+            if op == 'W':
+                filler = keep.tile([P, CHUNK], BF16, name="filler")
+                nc.vector.memset(filler[:], 0.0)
+                t = bank(5, [P, CHUNK], F32)
+                for n in range(int(arg)):
+                    nc.tensor.matmul(t[:], lhsT=filler[:, :P], rhs=filler[:], start=True, stop=True)
+                return
+            if op == 'K':
+                channel_constants()
+                return
+            if op == 'P':
+                perm[arg] = permute(src_of(arg), 'v')
+                return
+            if op in ('Ta', 'Tb'):
+                turn(arg, 'ab'.index(op[1]))
+                return
+            if op in ('aa', 'ab', 'va', 'vb'):
+                evacuate(arg, 'ab'.index(op[1]), op[0])
+                return
+            if op == 'Q':
+                assert (arg, 0, 'done') in turned and (arg, 1, 'done') in turned
+                if arg in w_raw:
+                    wq[arg] = quantise("w_" + arg, grouped[arg], E4M3)
+                else:
+                    xq[int(arg)] = quantise("x_" + arg, grouped[arg], E5M2)
+                return
+            if op == 'Md' or op == 'Mp':
+                name = 'dt' if op == 'Md' else 'ph'
+                product(name, int(arg), (ZDT if op == 'Md' else ZPH)[int(arg) // TILES])
+                return
+            j0, j1 = 0, TILES
+            if '.' in arg:
+                arg, hf = arg.split('.')
+                j0, j1 = 2 * int(hf), 2 * int(hf) + 2
+            h = slice(j0 * P, j1 * P)
             a = [int(v) for v in arg.split('-')]
             c = a[0]
             s = cs(*a)
+            if j1 - j0 < TILES:
+                s = slice(c * CHUNK + j0 * P, c * CHUNK + j1 * P)
             if op == 'e':
                 nc.scalar.activation(out=soft[:, s], in_=z['dt', c][:], func=ACT.Exp, bias=bias_dt)
             elif op == 'th':
@@ -221,8 +276,8 @@ def tile_mamba3mimoblock_pa_kernel(tc, x, state_re, state_im, W_dt, b_dt, W_ph, 
                                         in1=decay[:, s].unsqueeze(1).to_broadcast([P, 2, CHUNK]), op=ALU.mult)
                 work['r', c] = r
             elif op == 'B':
-                for g in range(PASSES):
-                    product('B', c, g, LATE[c][1])
+                for j in range(TILES):
+                    product('B', c * TILES + j, LATE[c][1])
             elif op == 'pS':
                 t = late.tile([P, 2, CHUNK], F32, name="by_sine")
                 src = work['r', c][:] if ('r', c) in work else work['st', c][:].rearrange("p a j t -> p a (j t)")
@@ -243,13 +298,13 @@ def tile_mamba3mimoblock_pa_kernel(tc, x, state_re, state_im, W_dt, b_dt, W_ph, 
                     work['pC', c] = late.tile([P, 2, CHUNK], F32, name="by_cosine")
                 src = work['r', c][:] if ('r', c) in work else work['st', c][:].rearrange("p a j t -> p a (j t)")
                 if op == 'p1':
-                    nc.vector.tensor_tensor(out=work['pC', c][:, 0, :], in0=src[:, 0, :], in1=cosine[:, s], op=ALU.mult)
+                    nc.vector.tensor_tensor(out=work['pC', c][:, 0, h], in0=src[:, 0, h], in1=cosine[:, s], op=ALU.mult)
                 elif op == 'p4':
-                    nc.vector.tensor_tensor(out=work['pC', c][:, 1, :], in0=src[:, 1, :], in1=cosine[:, s], op=ALU.mult)
+                    nc.vector.tensor_tensor(out=work['pC', c][:, 1, h], in0=src[:, 1, h], in1=cosine[:, s], op=ALU.mult)
                 elif op == 'p3':
-                    nc.vector.tensor_tensor(out=work['pS', c][:, 0, :], in0=src[:, 0, :], in1=sine[:, s], op=ALU.mult)
+                    nc.vector.tensor_tensor(out=work['pS', c][:, 0, h], in0=src[:, 0, h], in1=sine[:, s], op=ALU.mult)
                 elif ('cB', c) not in work:
-                    nc.vector.tensor_tensor(out=work['pS', c][:, 1, :], in0=src[:, 1, :], in1=sine[:, s], op=ALU.mult)
+                    nc.vector.tensor_tensor(out=work['pS', c][:, 1, h], in0=src[:, 1, h], in1=sine[:, s], op=ALU.mult)
                 else:
                     nc.vector.scalar_tensor_tensor(out=work['pS', c][:, 1, :], in0=src[:, 1, :], scalar=-1.0, in1=sine[:, s], op0=ALU.mult, op1=ALU.mult)
             elif op in ('Td', 'TS', 'TC'):
@@ -264,7 +319,7 @@ def tile_mamba3mimoblock_pa_kernel(tc, x, state_re, state_im, W_dt, b_dt, W_ph, 
                     tok = slice(j * P, (j + 1) * P)
                     for g in range(PASSES):
                         cols = slice(g * P, (g + 1) * P)
-                        nc.tensor.matmul_mx(out=t[:, j, :], lhsT=xq[c, g][0][:, tok].bitcast(E5M2), lhsT_scale=xq[c, g][1][:, tok],
+                        nc.tensor.matmul_mx(out=t[:, j, :], lhsT=xq[c * TILES + j][0][:, cols].bitcast(E5M2), lhsT_scale=xq[c * TILES + j][1][:, cols],
                                             rhs=wq['B'][0][:, cols].bitcast(E4M3), rhs_scale=wq['B'][1][:, cols], start=(g == 0), stop=(g == PASSES - 1))
                 work[op, c] = t
             elif op == 'rt':
@@ -307,8 +362,10 @@ def tile_mamba3mimoblock_pa_kernel(tc, x, state_re, state_im, W_dt, b_dt, W_ph, 
                 nc.vector.tensor_tensor(out=cosine[:, s], in0=cosine[:, s], in1=decay[:, s], op=ALU.mult)
             elif op == 'ore' or op == 'oim':
                 part = 0 if op == 'ore' else 1
-                t = bank(LATE[c][2 + part], [P, TILES, P], F32)
-                for j in range(TILES):
+                if j0 == 0:
+                    work[op, c] = bank(LATE[c][2 + part], [P, TILES, P], F32)
+                t = work[op, c]
+                for j in range(j0, j1):
                     tok = slice(j * P, (j + 1) * P)
                     with_b = part == 0 and ('cB', c) in work
                     if with_b:
@@ -316,47 +373,20 @@ def tile_mamba3mimoblock_pa_kernel(tc, x, state_re, state_im, W_dt, b_dt, W_ph, 
                     nc.tensor.matmul(t[:, j, :], lhsT=work['pS', c][:, 1 - part, tok], rhs=ident_f32[:], start=not with_b, stop=False, is_transpose=True)
                     nc.tensor.matmul(t[:, j, :], lhsT=work['pC', c][:, part, tok], rhs=ident_f32[:], start=False, stop=True, is_transpose=True)
                 work[op, c] = t
-            elif op == 'xre' or op == 'xim':
-                part = 0 if op == 'xre' else 1
-                res = late.tile([P, TILES, R], F32, name="result%d" % part)
-                src = work['o' + op[1:], c]
-                if EVAC[2 * c + part] == 'a':
-                    nc.scalar.copy(out=res[:], in_=src[:])
+            elif op in ('xre', 'xim', 'yre', 'yim'):
+                part = 0 if op[1:] == 're' else 1
+                if j0 == 0:
+                    work['res', part, c] = late.tile([P, TILES, R], F32, name="result%d" % part)
+                res = work['res', part, c][:, j0:j1]
+                src = work['o' + op[1:], c][:, j0:j1]
+                if op[0] == 'x':
+                    nc.scalar.copy(out=res, in_=src)
                 else:
-                    nc.vector.tensor_copy(out=res[:], in_=src[:])
+                    nc.vector.tensor_copy(out=res, in_=src)
                 dst = (out_0, out_1)[part][c * CHUNK:(c + 1) * CHUNK, :]
-                nc.sync.dma_start(out=dst.rearrange("(p j) r -> p j r", j=TILES), in_=res[:])
+                nc.sync.dma_start(out=dst.rearrange("(p j) r -> p j r", j=TILES)[:, j0:j1], in_=res)
             else:
                 raise ValueError(op)
 
-        seq = [('dt',), (0, 0), ('ph',)] + [divmod(i, PASSES) for i in range(1, UNITS)]
-        seq = seq[:WB_AT] + [('B',)] + seq[WB_AT:]
-        def src_of(item):
-            return w_source(item[0]) if len(item) == 1 else x_raw[item]
-        perm = {}
-        grouped = {}
-        pending = []
-        for i in range(-1, len(seq) + 2):
-            if i + 1 < len(seq) and i + 1 < len(PERM) and PERM[i + 1] != '-':
-                perm[i + 1] = permute(src_of(seq[i + 1]), PERM[i + 1])
-            if 0 <= i < len(seq) and i not in QFIRST:
-                grouped[i] = turn(src_of(seq[i]), perm.get(i))
-            if 0 <= i - 1 < len(seq):
-                item = seq[i - 1]
-                if len(item) == 1:
-                    wq[item[0]] = quantise("w_" + item[0], grouped[i - 1], E4M3)
-                else:
-                    xq[item] = quantise("x_%d_%d" % item, grouped[i - 1], E5M2)
-            if 0 <= i < len(seq) and i in QFIRST:
-                grouped[i] = turn(src_of(seq[i]), perm.get(i))
-            if i == CONST_AT:
-                channel_constants()
-            if 0 <= i - 2 < len(seq) and len(seq[i - 2]) == 2:
-                pending.append(seq[i - 2])
-            if i >= 4 and (len(pending) >= MXRUN or i >= len(seq)):
-                for c, g in pending:
-                    product("dt", c, g, ZDT[c])
-                    product("ph", c, g, ZPH[c])
-                pending = []
-            for what in SCHED.get(str(i), '').split():
-                do(what)
+        for what in ORDER.split():
+            do(what)

@@ -31,7 +31,7 @@ SCHED = {}
 XBANKS = [0, 1, 2, 3]
 ZDT = [4,5,7,4]
 ZPH = [6,6,6,5]
-LATE = [[0,6,0,1],[1,5,2,3],[2,7,0,1],[3,4,2,3]]
+LATE = [[0, 1, 0, 1], [2, 3, 2, 3], [0, 1, 0, 1], [2, 3, 2, 3]]
 EVAC = 'aaaaaaaa'
 MXRUN = 1
 WB_AT = 99
@@ -39,9 +39,10 @@ PERM = ''
 Q_MODE = 'q'
 D_MODE = 'r'
 XBUFS = 4
-ORDER = "L:wdt L:x0 L:wph L:x1 L:x2 L:x3 L:x4 L:x5 P:dt P:0 Ta:dt aa:dt Tb:dt ab:dt L:x6 P:ph Ta:0 aa:0 Tb:0 ab:0 Q:dt L:x7 P:1 Ta:ph aa:ph Tb:ph ab:ph Q:0 L:x8 P:2 Ta:1 aa:1 Tb:1 ab:1 Q:ph L:x9 L:s0 L:s1 K:0 P:3 Ta:2 aa:2 Tb:2 ab:2 Q:1 L:x10 Md:0 Mp:0 P:4 Ta:3 aa:3 Tb:3 ab:3 Q:2 L:x11 Md:1 Mp:1 P:5 Ta:4 aa:4 Tb:4 ab:4 Q:3 L:x12 Md:2 Mp:2 P:6 Ta:5 aa:5 Tb:5 ab:5 Q:4 L:x13 Md:3 Mp:3 e:0 th:0 min:0 P:7 Ta:6 aa:6 Tb:6 ab:6 Q:5 L:x14 Md:4 Mp:4 P:8 Ta:7 aa:7 Tb:7 ab:7 Q:6 L:x15 Md:5 Mp:5 P:9 Q:7 Ta:8 aa:8 Tb:8 ab:8 L:wB Md:6 Mp:6 Ta:9 va:9 Tb:9 ab:9 Q:8 Md:7 Mp:7 e:1 th:1 Ta:10 va:10 Tb:10 ab:10 Q:9 Md:8 Mp:8 min:1 ln:0 Ta:11 va:11 Tb:11 ab:11 Q:10 Md:9 Mp:9 ln:1 dt:0 Ta:12 va:12 Tb:12 ab:12 Q:11 Md:10 Mp:10 dt:1 d:0 Ta:13 va:13 Tb:13 ab:13 Q:12 Md:11 Mp:11 T:0 d:1 e:2 Ta:14 va:14 Tb:14 ab:14 Q:13 Md:12 Mp:12 T:1 th:2 min:2 n:0-1 Ta:15 va:15 Tb:15 ab:15 Q:14 Md:13 Mp:13 Q:15 Ta:B aa:B Tb:B ab:B Md:14 Mp:14 Q:B Md:15 Mp:15 e:3 th:3 st:0 st:1 st:2 st:3 B:0 B:1 f:0-1 min:3 r:0 ln:2 ln:3 r:1 dt:2 dt:3 B:2 B:3 d:2 d:3 T:2 T:3 n:2 n:3 r:2 f:2-3 S:0 abs:0 S:1 C:0 abs:1 C:1 r:3 pS:0 pC:0 oim:0 q:0 ore:0 S:2 abs:2 S:3 C:2 abs:3 C:3 pS:1 pC:1 oim:1 q:1 ore:1 xim:0 xre:0 pS:2 pC:2 oim:2 q:2 ore:2 xim:1 xre:1 p2:3 p1:3 q:3 ore:3 p3:3 p4:3 oim:3 xim:2 xre:2 xre:3 xim:3"
+PBUFS = 2
+ORDER = "L:wdt L:x0 L:wph L:x1 L:x2 L:x3 L:x4 L:x5 P:dt P:0 Ta:dt aa:dt Tb:dt ab:dt L:x6 P:ph Ta:0 aa:0 Tb:0 ab:0 Q:dt L:x7 P:1 Ta:ph aa:ph Tb:ph ab:ph Q:0 L:x8 P:2 Ta:1 aa:1 Tb:1 ab:1 Q:ph L:x9 L:s0 L:s1 K:0 P:3 Ta:2 aa:2 Tb:2 ab:2 Q:1 L:x10 Md:0 Mp:0 P:4 Ta:3 aa:3 Tb:3 ab:3 Q:2 L:x11 Md:1 Mp:1 P:5 Ta:4 aa:4 Tb:4 ab:4 Q:3 L:x12 Md:2 Mp:2 P:6 Ta:5 aa:5 Tb:5 ab:5 Q:4 L:x13 Md:3 Mp:3 e:0 th:0 min:0 P:7 Ta:6 aa:6 Tb:6 ab:6 Q:5 L:x14 Md:4 Mp:4 P:8 Ta:7 aa:7 Tb:7 ab:7 Q:6 L:x15 Md:5 Mp:5 P:9 Q:7 Ta:8 aa:8 Tb:8 ab:8 L:wB Md:6 Mp:6 Ta:9 va:9 Tb:9 ab:9 Q:8 Md:7 Mp:7 e:1 th:1 Ta:10 va:10 Tb:10 ab:10 Q:9 Md:8 Mp:8 min:1 ln:0 Ta:11 va:11 Tb:11 ab:11 Q:10 Md:9 Mp:9 ln:1 dt:0 Ta:12 va:12 Tb:12 ab:12 Q:11 Md:10 Mp:10 dt:1 d:0 Ta:13 va:13 Tb:13 ab:13 Q:12 Md:11 Mp:11 T:0 d:1 e:2 Ta:14 va:14 Tb:14 ab:14 Q:13 Md:12 Mp:12 T:1 th:2 min:2 n:0-1 Ta:15 va:15 Tb:15 ab:15 Q:14 Md:13 Mp:13 Q:15 Ta:B aa:B Tb:B ab:B Md:14 Q:B Md:15 Mp:14 Mp:15 e:3 Td:0 Td:1 Bt:0 Bt:1 f:0-1 min:3 rt:0 ln:2 ln:3 dt:2 dt:3 Bt:2 th:3 d:2 d:3 Td:2 T:2 rt:1 Td:3 Bt:3 T:3 n:2 n:3 rt:2 f:2-3 S:0 abs:0 TS:0 S:1 C:0 TC:0 abs:1 rt:3 S:2 C:1 mS:0 TS:1 TC:1 mC:0 mq:0 gim:0 gre:0 abs:2 S:3 C:2 abs:3 C:3 TS:2 TC:2 mS:1 mC:1 mq:1 gim:1 gre:1 TS:3 TC:3 mS:2 mC:2 mq:2 gim:2 gre:2 mS:3 mC:3 mq:3 vim:3 vre:3"
 PIN = 'all'
-MIX = []
+MIX = [[0,3,5,6],[1,0,1,2],[0,3,5,7],[1,0,1,4]]
 QFIRST = []
 CONST_AT = 3
 QBUFS = 8
@@ -100,7 +101,7 @@ def tile_mamba3mimoblock_pa_kernel(tc, x, state_re, state_im, W_dt, b_dt, W_ph, 
         counter = [0]
 
         def permute(source, eng):
-            t = stage.tile([P, 4, 2, P], F32, name="permuted", bufs=2)
+            t = stage.tile([P, 4, 2, P], F32, name="permuted", bufs=PBUFS)
             src = source.bitcast(F32).rearrange("p s (w u) -> p s u w", u=2)
             if eng == 'a':
                 nc.scalar.copy(out=t[:], in_=src)
@@ -193,8 +194,10 @@ def tile_mamba3mimoblock_pa_kernel(tc, x, state_re, state_im, W_dt, b_dt, W_ph, 
                 load(arg)
                 return
             if op == 'W':
-                filler = keep.tile([P, CHUNK], BF16, name="filler")
-                nc.vector.memset(filler[:], 0.0)
+                if 'filler' not in work:
+                    work['filler'] = keep.tile([P, CHUNK], BF16, name="filler")
+                    nc.vector.memset(work['filler'][:], 0.0)
+                filler = work['filler']
                 t = bank(5, [P, CHUNK], F32)
                 for n in range(int(arg)):
                     nc.tensor.matmul(t[:], lhsT=filler[:, :P], rhs=filler[:], start=True, stop=True)

import math
from contextlib import ExitStack

import concourse.mybir as mybir
from concourse.masks import make_identity

B, D, R = 2048, 2048, 128
FLOPS = 2 * B * D * 3 * R

F32 = mybir.dt.float32
BF16 = mybir.dt.bfloat16
I32 = mybir.dt.int32
U32 = mybir.dt.uint32
U8 = mybir.dt.uint8
E4M3 = mybir.dt.float8_e4m3fn_x4
E5M2 = mybir.dt.float8_e5m2_x4
ACT = mybir.ActivationFunctionType
ALU = mybir.AluOpType

P = 128
K_PASS = 512
PASSES = D // K_PASS
CHUNK = 512
TILES = CHUNK // P
CHUNKS = B // CHUNK
UNITS = CHUNKS * PASSES
EXP_CAP = 2.0 ** 50
ROUND_EVEN = 1.5 * 2.0 ** 24
COPY_ENG = 'avavav' + 'av' * 16
SCHED = {}
XBANKS = [0, 1, 2, 3]
ZDT = [4,5,7,4]
ZPH = [6,6,6,5]
LATE = [[0, 1, 0, 1], [2, 3, 2, 3], [0, 1, 0, 1], [2, 3, 2, 3]]
EVAC = 'aaaaaaaa'
MXRUN = 1
WB_AT = 99
PERM = ''
Q_MODE = 'q'
D_MODE = 'r'
XBUFS = 4
PBUFS = 2
ORDER = "L:wdt L:x0 L:wph L:x1 L:x2 L:x3 L:x4 L:x5 P:dt P:0 Ta:dt aa:dt Tb:dt ab:dt L:x6 P:ph Ta:0 aa:0 Tb:0 ab:0 Q:dt L:x7 P:1 Ta:ph aa:ph Tb:ph ab:ph Q:0 L:x8 P:2 Ta:1 aa:1 Tb:1 ab:1 Q:ph L:x9 L:s0 L:s1 K:0 P:3 Ta:2 aa:2 Tb:2 ab:2 Q:1 L:x10 Md:0 Mp:0 P:4 Ta:3 aa:3 Tb:3 ab:3 Q:2 L:x11 Md:1 Mp:1 P:5 Ta:4 aa:4 Tb:4 ab:4 Q:3 L:x12 Md:2 Mp:2 P:6 Ta:5 aa:5 Tb:5 ab:5 Q:4 L:x13 Md:3 Mp:3 e:0 th:0 min:0 P:7 Ta:6 aa:6 Tb:6 ab:6 Q:5 L:x14 Md:4 Mp:4 P:8 Ta:7 aa:7 Tb:7 ab:7 Q:6 L:x15 Md:5 Mp:5 P:9 Q:7 Ta:8 aa:8 Tb:8 ab:8 L:wB Md:6 Mp:6 Ta:9 va:9 Tb:9 ab:9 Q:8 Md:7 Mp:7 e:1 th:1 Ta:10 va:10 Tb:10 ab:10 Q:9 Md:8 Mp:8 min:1 ln:0 Ta:11 va:11 Tb:11 ab:11 Q:10 Md:9 Mp:9 ln:1 dt:0 Ta:12 va:12 Tb:12 ab:12 Q:11 Md:10 Mp:10 dt:1 d:0 Ta:13 va:13 Tb:13 ab:13 Q:12 Md:11 Mp:11 T:0 d:1 e:2 Ta:14 va:14 Tb:14 ab:14 Q:13 Md:12 Mp:12 T:1 th:2 min:2 n:0-1 Ta:15 va:15 Tb:15 ab:15 Q:14 Md:13 Mp:13 Q:15 Ta:B aa:B Tb:B ab:B Md:14 Q:B Md:15 Mp:14 Mp:15 e:3 Td:0 Td:1 Bt:0 Bt:1 f:0-1 min:3 rt:0 ln:2 ln:3 dt:2 dt:3 Bt:2 th:3 d:2 d:3 Td:2 T:2 rt:1 Td:3 Bt:3 T:3 n:2 n:3 rt:2 f:2-3 S:0 abs:0 TS:0 S:1 C:0 TC:0 abs:1 rt:3 S:2 C:1 mS:0 TS:1 TC:1 mC:0 mq:0 gim:0 gre:0 abs:2 S:3 C:2 abs:3 C:3 TS:2 TC:2 mS:1 mC:1 mq:1 gim:1 gre:1 TS:3 TC:3 mS:2 mC:2 mq:2 gim:2 gre:2 mS:3 mC:3 mq:3 vim:3 vre:3"
PIN = 'all'
MIX = [[0,3,5,6],[1,0,1,2],[0,3,5,7],[1,0,1,4]]
QFIRST = []
CONST_AT = 3
QBUFS = 8
LOADS = ''
RBUFS = 4


def tile_mamba3mimoblock_pa_kernel(tc, x, state_re, state_im, W_dt, b_dt, W_ph, b_ph, W_B, A_real, A_imag, out_0, out_1):
    nc = tc.nc
    with ExitStack() as ctx:
        keep = ctx.enter_context(tc.tile_pool(name="keep", bufs=1))
        stage = ctx.enter_context(tc.tile_pool(name="stage", bufs=4))
        late = ctx.enter_context(tc.tile_pool(name="late", bufs=2))
        psum = ctx.enter_context(tc.psum_pool(name="psum", bufs=1))
        if PIN == 'all':
            ctx.enter_context(tc.manual_schedule())
        else:
            ctx.enter_context(tc.manual_schedule(engines={mybir.EngineType.Activation, mybir.EngineType.PE, mybir.EngineType.SP}))

        def bank(index, shape, dtype):
            return psum.tile(shape, dtype, name="bank%d" % index, tag="bank%d" % index)

        w_raw = {}
        x_raw = {}

        def load_w(name, w):
            w_raw[name] = stage.tile([P, D], BF16, name="raw_" + name, tag="quarter", bufs=QBUFS)
            nc.sync.dma_start(out=w_raw[name][:], in_=w)

        def load_x(i):
            c, j = divmod(i, TILES)
            x_raw[i] = stage.tile([P, D], BF16, name="x_%d" % i, tag="quarter", bufs=QBUFS)
            rows = x[c * CHUNK:(c + 1) * CHUNK, :].rearrange("(p j) k -> j p k", j=TILES)
            nc.sync.dma_start(out=x_raw[i][:], in_=rows[j])

        ident_f32 = keep.tile([P, P], F32, name="ident_f32")
        ident_bf16 = keep.tile([P, P], BF16, name="ident_bf16")
        rows4 = keep.tile([P, P], BF16, name="rows4")
        nc.vector.memset(rows4[:], 0.0)
        make_identity(nc, ident_f32[:])
        nc.vector.tensor_copy(out=ident_bf16[:], in_=ident_f32[:])
        for i, vec in enumerate((b_dt, b_ph, A_real, A_imag)):
            nc.scalar.dma_start(out=rows4[i:i + 1, :], in_=vec.rearrange("(o r) -> o r", o=1))

        state = keep.tile([P, 2, CHUNKS, TILES, R], BF16, name="state")

        def load(item):
            if item[0] == 'w':
                load_w(item[1:], {'dt': W_dt, 'ph': W_ph, 'B': W_B}[item[1:]])
            elif item[0] == 's':
                part = int(item[1])
                nc.sync.dma_start(out=state[:, part], in_=(state_re, state_im)[part].rearrange("(c p j) r -> p c j r", p=P, j=TILES))
            else:
                load_x(int(item[1:]))

        counter = [0]

        def permute(source, eng):
            t = stage.tile([P, 4, 2, P], F32, name="permuted", bufs=PBUFS)
            src = source.bitcast(F32).rearrange("p s (w u) -> p s u w", u=2)
            if eng == 'a':
                nc.scalar.copy(out=t[:], in_=src)
            else:
                nc.vector.tensor_copy(out=t[:], in_=src)
            return t

        grouped = {}
        perm = {}
        turned = {}

        def src_of(item):
            raw = w_raw[item] if item in w_raw else x_raw[int(item)]
            return raw[:].rearrange("p (g k) -> p g k", g=PASSES)

        def turn(item, half):
            n = counter[0]
            counter[0] = n + 1
            xt = bank(XBANKS[n % len(XBANKS)], [P, 2, 2, P], F32)
            for s in range(2):
                for u in range(2):
                    if item in perm:
                        nc.tensor.transpose(xt[:, s, u, :], perm[item][:, 2 * half + s, u, :], ident_f32[:])
                    else:
                        words = src_of(item)[:, 2 * half + s, :].bitcast(F32)
                        nc.tensor.transpose(xt[:, s, u, :], words[:, u::2], ident_f32[:])
            turned[item, half] = xt

        def evacuate(item, half, eng):
            if item not in grouped:
                grouped[item] = stage.tile([P, 4 * P * 4], BF16, name="grouped", align_bytes=64)
            words_out = grouped[item][:].bitcast(F32).rearrange("p (s r u) -> p s r u", s=4, u=2)
            src = turned[item, half][:].rearrange("p s u r -> p s r u")
            dst = words_out[:, 2 * half:2 * half + 2]
            if eng == 'a':
                nc.scalar.copy(out=dst, in_=src)
            else:
                nc.vector.tensor_copy(out=dst, in_=src)
            turned[item, half, 'done'] = True

        def quantise(name, grouped, fmt):
            codes = keep.tile([P, 4 * P], U32, name="codes_" + name, align_bytes=64)
            scales = keep.tile([P, 4 * P], U8, name="scales_" + name, align_bytes=64)
            nc.vector.quantize_mx(out=codes[:].bitcast(fmt), scales=scales[:], in_=grouped[:])
            return codes, scales

        wq = {}
        work = {}
        xq = {}
        z = {}

        def product(name, i, index):
            c, j = divmod(i, TILES)
            if (name, c) not in z:
                z[name, c] = bank(index, [P, CHUNK], F32)
            for g in range(PASSES):
                cols = slice(g * P, (g + 1) * P)
                nc.tensor.matmul_mx(out=z[name, c][:, j * P:(j + 1) * P], lhsT=wq[name][0][:, cols].bitcast(E4M3), lhsT_scale=wq[name][1][:, cols],
                                    rhs=xq[i][0][:, cols].bitcast(E5M2), rhs_scale=xq[i][1][:, cols], start=(g == 0), stop=(g == PASSES - 1))
            work[name, 'n', c] = work.get((name, 'n', c), 0) + 1

        def w_source(name):
            return w_raw[name][:].rearrange("p (g k) -> p g k", g=PASSES)

        consts = keep.tile([P, 8], F32, name="consts")
        bias_dt, bias_ph, neg_rate, half_turns = consts[:, 0:1], consts[:, 1:2], consts[:, 4:5], consts[:, 5:6]

        def channel_constants():
            t = bank(7, [P, P], BF16)
            nc.tensor.transpose(t[:], rows4[:], ident_bf16[:])
            nc.vector.tensor_copy(out=consts[:, 0:4], in_=t[:, 0:4])
            nc.scalar.activation(out=consts[:, 6:7], in_=consts[:, 2:3], func=ACT.Exp)
            nc.vector.tensor_scalar(out=half_turns, in0=consts[:, 3:4], scalar1=1.0 / math.pi, scalar2=None, op0=ALU.mult)
            nc.vector.tensor_scalar(out=neg_rate, in0=consts[:, 6:7], scalar1=-1.0, scalar2=None, op0=ALU.mult)

        soft = keep.tile([P, B], F32, name="soft")
        step = keep.tile([P, B], F32, name="step")
        turns = keep.tile([P, B], F32, name="turns")
        whole = keep.tile([P, B], I32, name="whole")
        sine = keep.tile([P, B], F32, name="sine")
        cosine = keep.tile([P, B], F32, name="cosine")
        decay = soft

        def cs(c0, c1=None):
            return slice(c0 * CHUNK, ((c0 if c1 is None else c1) + 1) * CHUNK)

        def do(what):
            op, arg = what.split(':')
            if op == 'L':
                load(arg)
                return
            if op == 'W':
                if 'filler' not in work:
                    work['filler'] = keep.tile([P, CHUNK], BF16, name="filler")
                    nc.vector.memset(work['filler'][:], 0.0)
                filler = work['filler']
                t = bank(5, [P, CHUNK], F32)
                for n in range(int(arg)):
                    nc.tensor.matmul(t[:], lhsT=filler[:, :P], rhs=filler[:], start=True, stop=True)
                return
            if op == 'K':
                channel_constants()
                return
            if op == 'P':
                perm[arg] = permute(src_of(arg), 'v')
                return
            if op in ('Ta', 'Tb'):
                turn(arg, 'ab'.index(op[1]))
                return
            if op in ('aa', 'ab', 'va', 'vb'):
                evacuate(arg, 'ab'.index(op[1]), op[0])
                return
            if op == 'Q':
                assert (arg, 0, 'done') in turned and (arg, 1, 'done') in turned
                if arg in w_raw:
                    wq[arg] = quantise("w_" + arg, grouped[arg], E4M3)
                else:
                    xq[int(arg)] = quantise("x_" + arg, grouped[arg], E5M2)
                return
            if op == 'Md' or op == 'Mp':
                name = 'dt' if op == 'Md' else 'ph'
                product(name, int(arg), (ZDT if op == 'Md' else ZPH)[int(arg) // TILES])
                return
            j0, j1 = 0, TILES
            if '.' in arg:
                arg, hf = arg.split('.')
                j0, j1 = 2 * int(hf), 2 * int(hf) + 2
            h = slice(j0 * P, j1 * P)
            a = [int(v) for v in arg.split('-')]
            c = a[0]
            s = cs(*a)
            if j1 - j0 < TILES:
                s = slice(c * CHUNK + j0 * P, c * CHUNK + j1 * P)
            if op == 'e':
                nc.scalar.activation(out=soft[:, s], in_=z['dt', c][:], func=ACT.Exp, bias=bias_dt)
            elif op == 'th':
                nc.scalar.activation(out=turns[:, s], in_=z['ph', c][:], func=ACT.Tanh, bias=bias_ph)
            elif op == 'min':
                nc.vector.tensor_scalar(out=soft[:, s], in0=soft[:, s], scalar1=EXP_CAP, scalar2=None, op0=ALU.min)
            elif op == 'ln':
                nc.scalar.activation(out=soft[:, s], in_=soft[:, s], func=ACT.Ln, bias=1.0)
            elif op == 'dt':
                nc.vector.scalar_tensor_tensor(out=step[:, s], in0=z['dt', c][:], scalar=bias_dt, in1=soft[:, s], op0=ALU.add, op1=ALU.max)
            elif op == 'T':
                nc.vector.scalar_tensor_tensor(out=turns[:, s], in0=step[:, s], scalar=half_turns, in1=turns[:, s], op0=ALU.mult, op1=ALU.add)
            elif op == 'n':
                nc.vector.tensor_scalar(out=whole[:, s], in0=turns[:, s], scalar1=ROUND_EVEN, scalar2=ROUND_EVEN, op0=ALU.add, op1=ALU.subtract)
            elif op == 'an':
                nc.scalar.activation(out=whole[:, s].bitcast(U32), in_=turns[:, s], func=ACT.Copy, bias=ROUND_EVEN)
            elif op == 'fa':
                nc.vector.scalar_tensor_tensor(out=turns[:, s], in0=whole[:, s], scalar=ROUND_EVEN, in1=turns[:, s], op0=ALU.subtract, op1=ALU.subtract)
                for v in range(a[0], a[-1] + 1):
                    work['neg', v] = True
            elif op == 'f':
                nc.vector.tensor_tensor(out=turns[:, s], in0=turns[:, s], in1=whole[:, s], op=ALU.subtract)
            elif op == 'd':
                nc.scalar.activation(out=decay[:, s], in_=step[:, s], func=ACT.Exp, scale=neg_rate)
            elif op == 'abs':
                nc.scalar.activation(out=cosine[:, s], in_=turns[:, s], func=ACT.Abs)
            elif op == 'vabs':
                nc.vector.scalar_tensor_tensor(out=cosine[:, s], in0=turns[:, s], scalar=-1.0, in1=turns[:, s], op0=ALU.mult, op1=ALU.max)
            elif op == 'S':
                nc.scalar.activation(out=sine[:, s], in_=turns[:, s], func=ACT.Sin, scale=-math.pi if ('neg', c) in work else math.pi)
            elif op == 'C':
                nc.scalar.activation(out=cosine[:, s], in_=cosine[:, s], func=ACT.Sin, scale=-math.pi, bias=math.pi / 2)
            elif op == 'st':
                t = bank(LATE[c][0], [P, 2, TILES, P], BF16)
                for part in range(2):
                    for j in range(TILES):
                        nc.tensor.transpose(t[:, part, j, :], state[:, part, c, j, :], ident_bf16[:])
                work['st', c] = t
            elif op == 'r':
                r = late.tile([P, 2, CHUNK], F32, name="damped", bufs=RBUFS)
                nc.vector.tensor_tensor(out=r[:], in0=work['st', c][:].rearrange("p a j t -> p a (j t)"),
                                        in1=decay[:, s].unsqueeze(1).to_broadcast([P, 2, CHUNK]), op=ALU.mult)
                work['r', c] = r
            elif op == 'B':
                for j in range(TILES):
                    product('B', c * TILES + j, LATE[c][1])
            elif op == 'pS':
                t = late.tile([P, 2, CHUNK], F32, name="by_sine")
                src = work['r', c][:] if ('r', c) in work else work['st', c][:].rearrange("p a j t -> p a (j t)")
                if Q_MODE == 'q':
                    nc.vector.tensor_tensor(out=t[:], in0=src, in1=sine[:, s].unsqueeze(1).to_broadcast([P, 2, CHUNK]), op=ALU.mult)
                else:
                    nc.vector.tensor_tensor(out=t[:, 0, :], in0=src[:, 0, :], in1=sine[:, s], op=ALU.mult)
                    nc.vector.scalar_tensor_tensor(out=t[:, 1, :], in0=src[:, 1, :], scalar=-1.0, in1=sine[:, s], op0=ALU.mult, op1=ALU.mult)
                work['pS', c] = t
            elif op == 'pC':
                t = late.tile([P, 2, CHUNK], F32, name="by_cosine")
                src = work['r', c][:] if ('r', c) in work else work['st', c][:].rearrange("p a j t -> p a (j t)")
                nc.vector.tensor_tensor(out=t[:], in0=src, in1=cosine[:, s].unsqueeze(1).to_broadcast([P, 2, CHUNK]), op=ALU.mult)
                work['pC', c] = t
            elif op in ('p1', 'p2', 'p3', 'p4'):
                if ('pS', c) not in work:
                    work['pS', c] = late.tile([P, 2, CHUNK], F32, name="by_sine")
                    work['pC', c] = late.tile([P, 2, CHUNK], F32, name="by_cosine")
                src = work['r', c][:] if ('r', c) in work else work['st', c][:].rearrange("p a j t -> p a (j t)")
                if op == 'p1':
                    nc.vector.tensor_tensor(out=work['pC', c][:, 0, h], in0=src[:, 0, h], in1=cosine[:, s], op=ALU.mult)
                elif op == 'p4':
                    nc.vector.tensor_tensor(out=work['pC', c][:, 1, h], in0=src[:, 1, h], in1=cosine[:, s], op=ALU.mult)
                elif op == 'p3':
                    nc.vector.tensor_tensor(out=work['pS', c][:, 0, h], in0=src[:, 0, h], in1=sine[:, s], op=ALU.mult)
                elif ('cB', c) not in work:
                    nc.vector.tensor_tensor(out=work['pS', c][:, 1, h], in0=src[:, 1, h], in1=sine[:, s], op=ALU.mult)
                else:
                    nc.vector.scalar_tensor_tensor(out=work['pS', c][:, 1, :], in0=src[:, 1, :], scalar=-1.0, in1=sine[:, s], op0=ALU.mult, op1=ALU.mult)
            elif op in ('Td', 'TS', 'TC'):
                src = {'Td': decay, 'TS': sine, 'TC': cosine}[op]
                t = bank(MIX[c][('Td', 'TS', 'TC').index(op)], [P, TILES, P], F32)
                for j in range(TILES):
                    nc.tensor.transpose(t[:, j, :], src[:, c * CHUNK + j * P:c * CHUNK + (j + 1) * P], ident_f32[:])
                work[op, c] = t
            elif op == 'Bt':
                t = bank(MIX[c][3], [P, TILES, P], F32)
                for j in range(TILES):
                    tok = slice(j * P, (j + 1) * P)
                    for g in range(PASSES):
                        cols = slice(g * P, (g + 1) * P)
                        nc.tensor.matmul_mx(out=t[:, j, :], lhsT=xq[c * TILES + j][0][:, cols].bitcast(E5M2), lhsT_scale=xq[c * TILES + j][1][:, cols],
                                            rhs=wq['B'][0][:, cols].bitcast(E4M3), rhs_scale=wq['B'][1][:, cols], start=(g == 0), stop=(g == PASSES - 1))
                work[op, c] = t
            elif op == 'rt':
                r = late.tile([P, 2, CHUNK], F32, name="damped", bufs=RBUFS)
                nc.vector.tensor_tensor(out=r[:], in0=work['Td', c][:].rearrange("p j t -> p (j t)").unsqueeze(1).to_broadcast([P, 2, CHUNK]),
                                        in1=state[:, :, c].rearrange("p a j r -> p a (j r)"), op=ALU.mult)
                work['r', c] = r
            elif op == 'mS' or op == 'mC':
                t = late.tile([P, 2, CHUNK], F32, name="by_sine" if op == 'mS' else "by_cosine")
                nc.vector.tensor_tensor(out=t[:], in0=work['T' + op[1], c][:].rearrange("p j t -> p (j t)").unsqueeze(1).to_broadcast([P, 2, CHUNK]),
                                        in1=work['r', c][:], op=ALU.mult)
                work['p' + op[1], c] = t
            elif op == 'mq':
                t = work['pS', c]
                nc.vector.tensor_tensor(out=t[:, 1, :], in0=work['Bt', c][:].rearrange("p j t -> p (j t)"), in1=t[:, 1, :], op=ALU.subtract)
            elif op in ('gre', 'gim', 'vre', 'vim'):
                part = 0 if op[1:] == 're' else 1
                res = late.tile([P, CHUNK], F32, name="result%d" % part)
                eng = nc.gpsimd if op[0] == 'g' else nc.vector
                eng.tensor_tensor(out=res[:], in0=work['pS', c][:, 1 - part, :], in1=work['pC', c][:, part, :], op=ALU.add)
                dst = (out_0, out_1)[part][c * CHUNK:(c + 1) * CHUNK, :]
                nc.sync.dma_start(out=dst.rearrange("(p j) r -> p (j r)", j=TILES), in_=res[:])
            elif op == 'q':
                t = work['pS', c]
                nc.vector.tensor_tensor(out=t[:, 1, :], in0=z['B', c][:], in1=t[:, 1, :], op=ALU.subtract)
            elif op == 'cB' or op == 'vB':
                t = late.tile([P, CHUNK], F32, name="b_val", bufs=4)
                if op == 'cB':
                    nc.scalar.copy(out=t[:], in_=z['B', c][:])
                else:
                    nc.vector.tensor_copy(out=t[:], in_=z['B', c][:])
                work['cB', c] = t
            elif op == 'gS':
                nc.gpsimd.tensor_tensor(out=sine[:, s], in0=sine[:, s], in1=decay[:, s], op=ALU.mult)
            elif op == 'gC':
                nc.gpsimd.tensor_tensor(out=cosine[:, s], in0=cosine[:, s], in1=decay[:, s], op=ALU.mult)
            elif op == 'vS':
                nc.vector.tensor_tensor(out=sine[:, s], in0=sine[:, s], in1=decay[:, s], op=ALU.mult)
            elif op == 'vC':
                nc.vector.tensor_tensor(out=cosine[:, s], in0=cosine[:, s], in1=decay[:, s], op=ALU.mult)
            elif op == 'ore' or op == 'oim':
                part = 0 if op == 'ore' else 1
                if j0 == 0:
                    work[op, c] = bank(LATE[c][2 + part], [P, TILES, P], F32)
                t = work[op, c]
                for j in range(j0, j1):
                    tok = slice(j * P, (j + 1) * P)
                    with_b = part == 0 and ('cB', c) in work
                    if with_b:
                        nc.tensor.matmul(t[:, j, :], lhsT=work['cB', c][:, tok], rhs=ident_f32[:], start=True, stop=False, is_transpose=True)
                    nc.tensor.matmul(t[:, j, :], lhsT=work['pS', c][:, 1 - part, tok], rhs=ident_f32[:], start=not with_b, stop=False, is_transpose=True)
                    nc.tensor.matmul(t[:, j, :], lhsT=work['pC', c][:, part, tok], rhs=ident_f32[:], start=False, stop=True, is_transpose=True)
                work[op, c] = t
            elif op in ('xre', 'xim', 'yre', 'yim'):
                part = 0 if op[1:] == 're' else 1
                if j0 == 0:
                    work['res', part, c] = late.tile([P, TILES, R], F32, name="result%d" % part)
                res = work['res', part, c][:, j0:j1]
                src = work['o' + op[1:], c][:, j0:j1]
                if op[0] == 'x':
                    nc.scalar.copy(out=res, in_=src)
                else:
                    nc.vector.tensor_copy(out=res, in_=src)
                dst = (out_0, out_1)[part][c * CHUNK:(c + 1) * CHUNK, :]
                nc.sync.dma_start(out=dst.rearrange("(p j) r -> p j r", j=TILES)[:, j0:j1], in_=res)
            else:
                raise ValueError(op)

        for what in ORDER.split():
            do(what)
